import numpy as np
import ml_dtypes


def mxq(x, axis, fmt="e4m3"):
    dtype, down = {"e4m3": (ml_dtypes.float8_e4m3fn, 7), "e5m2": (ml_dtypes.float8_e5m2, 14)}[fmt]
    v = np.moveaxis(np.asarray(x, np.float32).astype(ml_dtypes.bfloat16).astype(np.float64), axis, -1)
    blocks = v.reshape(v.shape[:-1] + (-1, 32))
    amax = np.abs(blocks).max(-1, keepdims=True)
    byte = np.maximum(np.where(amax > 0, np.frexp(amax)[1] - 1 + 127, 0) - down, 1)
    scale = np.exp2(byte - 127.0)
    codes = (blocks / scale).astype(np.float32).astype(dtype).astype(np.float64)
    return np.moveaxis((codes * scale).reshape(v.shape), -1, axis)


WIDE = False


def mx_kscale(k):
    if not WIDE:
        return np.ones(k)
    levels = np.array([10, -10, 5, -5, 0])
    a = np.random.permutation(np.resize(levels, k // 512 * 4)).reshape(k // 512, 4)
    idx = np.arange(k)
    return np.exp2(a[idx // 512, idx % 128 // 32])


BF16 = ml_dtypes.bfloat16


def bf(x):
    return np.asarray(x, np.float32).astype(BF16)


def f64(x):
    return np.asarray(x).astype(np.float64)


T, K, N = 8192, 1024, 256
BLK = 32


def setup_inputs():
    s = np.repeat(np.asarray(mx_kscale(K))[::BLK], BLK)
    hi = s > 1.0
    lead = (np.arange(K) % BLK) == 0
    xr = np.random.standard_normal((T, K)) * 6.0 / np.sqrt(K)
    wr = np.random.standard_normal((N, K)) * np.sqrt(2.0 / K)
    xr = np.where(hi & lead, 0.0, np.where(hi, xr * 2.0**20, xr))
    wr = np.where(hi & ~lead, 0.0, wr)
    return {"x": bf(xr), "weight": bf(wr)}


def reference(x, weight):
    binary_weight = np.sign(f64(weight))
    return mxq(f64(x), 1, "e4m3") @ mxq(binary_weight, 1, "e4m3").T

@@ -1,0 +1,136 @@
+import concourse.mybir as mybir
+from concourse.masks import make_identity
+
+F32 = mybir.dt.float32
+BF16 = mybir.dt.bfloat16
+U32 = mybir.dt.uint32
+U8 = mybir.dt.uint8
+FP8X4 = mybir.dt.float8_e4m3fn_x4
+SIGN = mybir.ActivationFunctionType.Sign
+
+P = 128
+T, K, N = 8192, 1024, 256
+FLOPS = 2 * T * K * N
+TILES = T // P
+CH = 4
+CHUNKS = TILES // CH
+WORDS = K // 2
+X_BUFS = 12
+
+
+def tile_binarylinear_t_kernel(tc, x, weight, out):
+    nc = tc.nc
+    xv = x.rearrange("(p t) k -> p (t k)", t=TILES)
+    ov = out.rearrange("(p t) n -> p (t n)", t=TILES)
+    with tc.tile_pool(name="const", bufs=1) as const, tc.tile_pool(name="xin", bufs=X_BUFS) as xin, tc.tile_pool(
+        name="grp", bufs=2
+    ) as grp, tc.tile_pool(name="mx", bufs=3) as mx, tc.tile_pool(name="res", bufs=CHUNKS) as res, tc.psum_pool(
+        name="psum", bufs=4
+    ) as psum, tc.manual_schedule():
+        x_tiles = {}
+
+        def load(c):
+            x_sb = xin.tile([P, CH * K], BF16, name="x_sb", tag="x_sb")
+            nc.sync.dma_start(out=x_sb[:], in_=xv[:, c * CH * K : (c + 1) * CH * K])
+            x_tiles[c] = x_sb
+
+        w_sb = const.tile([P, 2 * K], BF16, name="w_sb")
+        nc.sync.dma_start(
+            out=w_sb[:].rearrange("p (j k) -> p j k", j=2),
+            in_=weight.rearrange("(j p) k -> p j k", p=P),
+        )
+        for c in range(X_BUFS):
+            load(c)
+
+        ident = const.tile([P, P], F32, name="ident")
+        make_identity(nc, ident[:])
+
+        w_words = w_sb[:].bitcast(F32)
+        w_grp = const.tile([P, 4 * 2 * N], BF16, name="w_grp", align_bytes=64)
+        w_codes = const.tile([P, 2 * N], U32, name="w_codes", align_bytes=64)
+        w_scales = const.tile([P, 2 * N], U8, name="w_scales", align_bytes=64)
+        w_grp_v = w_grp[:].rearrange("p (g n u e) -> p g n u e", g=2, n=N, u=2, e=2)
+        for jo in range(2):
+            wt = psum.tile([P, 512], F32, name="wt", tag="xt")
+            for j in range(4):
+                nc.tensor.transpose(
+                    wt[:, j * P : (j + 1) * P],
+                    w_words[:, jo * WORDS + j * P : jo * WORDS + (j + 1) * P],
+                    ident[:],
+                )
+            wt_v = wt[:].bitcast(BF16).rearrange("p (g u o e) -> p g o u e", g=2, u=2, o=P, e=2)
+            for g in range(2):
+                nc.scalar.activation(out=w_grp_v[:, g, jo * P : (jo + 1) * P, :, :], in_=wt_v[:, g], func=SIGN)
+        nc.vector.quantize_mx(out=w_codes[:].bitcast(FP8X4), scales=w_scales[:], in_=w_grp[:])
+
+        grouped = {}
+        codes = {}
+        scales = {}
+
+        def transposes(c):
+            x_words = x_tiles[c][:].bitcast(F32)
+            g_sb = grp.tile([P, CH * K], BF16, name="g_sb", tag="g_sb", align_bytes=64)
+            grouped[c] = g_sb
+            g_words = g_sb[:].bitcast(F32).rearrange("p (r g t u) -> p r g t u", r=CH, g=2, t=P, u=2)
+            banks = []
+            for r in range(CH):
+                xt = psum.tile([P, 512], F32, name="xt", tag="xt")
+                for j in range(4):
+                    nc.tensor.transpose(
+                        xt[:, j * P : (j + 1) * P],
+                        x_words[:, r * WORDS + j * P : r * WORDS + (j + 1) * P],
+                        ident[:],
+                    )
+                banks.append(xt)
+            for r in range(CH):
+                nc.scalar.copy(
+                    out=g_words[:, r],
+                    in_=banks[r][:].rearrange("p (g u t) -> p g t u", g=2, u=2, t=P),
+                )
+
+        def quantise(c, h):
+            if h == 0:
+                codes[c] = mx.tile([P, CH * K // 4], U32, name="codes", tag="codes", align_bytes=64)
+                scales[c] = mx.tile([P, CH * K // 4], U8, name="scales", tag="scales", align_bytes=64)
+            w = CH * K // 8
+            nc.vector.quantize_mx(
+                out=codes[c][:, h * w : (h + 1) * w].bitcast(FP8X4),
+                scales=scales[c][:, h * w : (h + 1) * w],
+                in_=grouped[c][:, h * 4 * w : (h + 1) * 4 * w],
+            )
+
+        def multiply(c):
+            accs = []
+            for b in range(CH // 2):
+                acc = psum.tile([P, 512], F32, name="acc", tag="acc")
+                for half in range(2):
+                    r = 2 * b + half
+                    for g in range(2):
+                        s = (r * 2 + g) * P
+                        nc.tensor.matmul_mx(
+                            out=acc[:, half * N : (half + 1) * N],
+                            lhsT=codes[c][:, s : s + P].bitcast(FP8X4),
+                            lhsT_scale=scales[c][:, s : s + P],
+                            rhs=w_codes[:, g * N : (g + 1) * N].bitcast(FP8X4),
+                            rhs_scale=w_scales[:, g * N : (g + 1) * N],
+                            start=(g == 0),
+                            stop=(g == 1),
+                        )
+                accs.append(acc)
+            return accs
+
+        for c in range(CHUNKS + 1):
+            if c < CHUNKS:
+                transposes(c)
+            accs = multiply(c - 1) if c >= 1 else None
+            if accs is not None:
+                o_sb = res.tile([P, CH * N], F32, name="o_sb", tag="o_sb")
+            for h in range(2):
+                if c < CHUNKS:
+                    quantise(c, h)
+                if accs is not None:
+                    nc.vector.tensor_copy(out=o_sb[:, h * 512 : (h + 1) * 512], in_=accs[h][:])
+            if c + X_BUFS < CHUNKS:
+                load(c + X_BUFS)
+            if accs is not None:
+                nc.sync.dma_start(out=ov[:, (c - 1) * CH * N : c * CH * N], in_=o_sb[:])

@@ -15,32 +15,44 @@ TILES = T // P
 CH = 4
 CHUNKS = TILES // CH
 WORDS = K // 2
-X_BUFS = 12
+LOADS = (4, 4, 4, 4, 8, 8, 8, 8, 16)
+STORES = (16, 16, 16, 8, 4, 4)
+assert sum(LOADS) == TILES and sum(STORES) == TILES
 
 
 def tile_binarylinear_t_kernel(tc, x, weight, out):
     nc = tc.nc
     xv = x.rearrange("(p t) k -> p (t k)", t=TILES)
     ov = out.rearrange("(p t) n -> p (t n)", t=TILES)
-    with tc.tile_pool(name="const", bufs=1) as const, tc.tile_pool(name="xin", bufs=X_BUFS) as xin, tc.tile_pool(
-        name="grp", bufs=2
-    ) as grp, tc.tile_pool(name="mx", bufs=3) as mx, tc.tile_pool(name="res", bufs=CHUNKS) as res, tc.psum_pool(
-        name="psum", bufs=4
-    ) as psum, tc.manual_schedule():
-        x_tiles = {}
-
-        def load(c):
-            x_sb = xin.tile([P, CH * K], BF16, name="x_sb", tag="x_sb")
-            nc.sync.dma_start(out=x_sb[:], in_=xv[:, c * CH * K : (c + 1) * CH * K])
-            x_tiles[c] = x_sb
-
+    with tc.tile_pool(name="const", bufs=1) as const, tc.tile_pool(name="grp", bufs=2) as grp, tc.tile_pool(
+        name="mx", bufs=2
+    ) as mx, tc.psum_pool(name="psum", bufs=4) as psum, tc.manual_schedule():
         w_sb = const.tile([P, 2 * K], BF16, name="w_sb")
-        nc.sync.dma_start(
-            out=w_sb[:].rearrange("p (j k) -> p j k", j=2),
-            in_=weight.rearrange("(j p) k -> p j k", p=P),
-        )
-        for c in range(X_BUFS):
-            load(c)
+
+        def load_w():
+            nc.sync.dma_start(
+                out=w_sb[:].rearrange("p (j k) -> p j k", j=2),
+                in_=weight.rearrange("(j p) k -> p j k", p=P),
+            )
+
+        x_words = {}
+        first = 0
+        for i, n in enumerate(LOADS):
+            if i == 0:
+                load_w()
+            x_sb = const.tile([P, n * K], BF16, name="x_sb%d" % i)
+            nc.sync.dma_start(out=x_sb[:], in_=xv[:, first * K : (first + n) * K])
+            for t in range(n):
+                x_words[first + t] = x_sb[:].bitcast(F32)[:, t * WORDS : (t + 1) * WORDS]
+            first += n
+
+        o_slot = {}
+        first = 0
+        for i, n in enumerate(STORES):
+            o_sb = const.tile([P, n * N], F32, name="o_sb%d" % i)
+            for t in range(n):
+                o_slot[first + t] = (o_sb, t, (first, n) if t == n - 1 else None)
+            first += n
 
         ident = const.tile([P, P], F32, name="ident")
         make_identity(nc, ident[:])
@@ -50,25 +62,26 @@ def tile_binarylinear_t_kernel(tc, x, weight, out):
         w_codes = const.tile([P, 2 * N], U32, name="w_codes", align_bytes=64)
         w_scales = const.tile([P, 2 * N], U8, name="w_scales", align_bytes=64)
         w_grp_v = w_grp[:].rearrange("p (g n u e) -> p g n u e", g=2, n=N, u=2, e=2)
-        for jo in range(2):
-            wt = psum.tile([P, 512], F32, name="wt", tag="xt")
-            for j in range(4):
-                nc.tensor.transpose(
-                    wt[:, j * P : (j + 1) * P],
-                    w_words[:, jo * WORDS + j * P : jo * WORDS + (j + 1) * P],
-                    ident[:],
-                )
-            wt_v = wt[:].bitcast(BF16).rearrange("p (g u o e) -> p g o u e", g=2, u=2, o=P, e=2)
-            for g in range(2):
-                nc.scalar.activation(out=w_grp_v[:, g, jo * P : (jo + 1) * P, :, :], in_=wt_v[:, g], func=SIGN)
-        nc.vector.quantize_mx(out=w_codes[:].bitcast(FP8X4), scales=w_scales[:], in_=w_grp[:])
+
+        def weights():
+            for jo in range(2):
+                wt = psum.tile([P, 512], F32, name="wt", tag="xt")
+                for j in range(4):
+                    nc.tensor.transpose(
+                        wt[:, j * P : (j + 1) * P],
+                        w_words[:, jo * WORDS + j * P : jo * WORDS + (j + 1) * P],
+                        ident[:],
+                    )
+                wt_v = wt[:].bitcast(BF16).rearrange("p (g u o e) -> p g o u e", g=2, u=2, o=P, e=2)
+                for g in range(2):
+                    nc.scalar.activation(out=w_grp_v[:, g, jo * P : (jo + 1) * P, :, :], in_=wt_v[:, g], func=SIGN)
+            nc.vector.quantize_mx(out=w_codes[:].bitcast(FP8X4), scales=w_scales[:], in_=w_grp[:])
 
         grouped = {}
         codes = {}
         scales = {}
 
         def transposes(c):
-            x_words = x_tiles[c][:].bitcast(F32)
             g_sb = grp.tile([P, CH * K], BF16, name="g_sb", tag="g_sb", align_bytes=64)
             grouped[c] = g_sb
             g_words = g_sb[:].bitcast(F32).rearrange("p (r g t u) -> p r g t u", r=CH, g=2, t=P, u=2)
@@ -76,11 +89,7 @@ def tile_binarylinear_t_kernel(tc, x, weight, out):
             for r in range(CH):
                 xt = psum.tile([P, 512], F32, name="xt", tag="xt")
                 for j in range(4):
-                    nc.tensor.transpose(
-                        xt[:, j * P : (j + 1) * P],
-                        x_words[:, r * WORDS + j * P : r * WORDS + (j + 1) * P],
-                        ident[:],
-                    )
+                    nc.tensor.transpose(xt[:, j * P : (j + 1) * P], x_words[c * CH + r][:, j * P : (j + 1) * P], ident[:])
                 banks.append(xt)
             for r in range(CH):
                 nc.scalar.copy(
@@ -119,18 +128,22 @@ def tile_binarylinear_t_kernel(tc, x, weight, out):
                 accs.append(acc)
             return accs
 
+        def copy_out(c, b, acc):
+            t = c * CH + 2 * b
+            o_sb, col, unused = o_slot[t]
+            nc.vector.tensor_copy(out=o_sb[:, col * N : (col + 2) * N], in_=acc[:])
+            store = o_slot[t + 1][2]
+            if store is not None:
+                nc.sync.dma_start(out=ov[:, store[0] * N : (store[0] + store[1]) * N], in_=o_sb[:])
+
+        weights()
         for c in range(CHUNKS + 1):
             if c < CHUNKS:
                 transposes(c)
+
             accs = multiply(c - 1) if c >= 1 else None
-            if accs is not None:
-                o_sb = res.tile([P, CH * N], F32, name="o_sb", tag="o_sb")
             for h in range(2):
                 if c < CHUNKS:
                     quantise(c, h)
                 if accs is not None:
-                    nc.vector.tensor_copy(out=o_sb[:, h * 512 : (h + 1) * 512], in_=accs[h][:])
-            if c + X_BUFS < CHUNKS:
-                load(c + X_BUFS)
-            if accs is not None:
-                nc.sync.dma_start(out=ov[:, (c - 1) * CH * N : c * CH * N], in_=o_sb[:])
+                    copy_out(c - 1, h, accs[h])

@@ -15,8 +15,8 @@ TILES = T // P
 CH = 4
 CHUNKS = TILES // CH
 WORDS = K // 2
-LOADS = (4, 4, 4, 4, 8, 8, 8, 8, 16)
-STORES = (16, 16, 16, 8, 4, 4)
+LOADS = (4, 4, 5, 7, 8, 10, 11, 15)
+STORES = (24, 24, 8, 4, 4)
 assert sum(LOADS) == TILES and sum(STORES) == TILES
 
 

import concourse.mybir as mybir
from concourse.masks import make_identity

F32 = mybir.dt.float32
BF16 = mybir.dt.bfloat16
U32 = mybir.dt.uint32
U8 = mybir.dt.uint8
FP8X4 = mybir.dt.float8_e4m3fn_x4
SIGN = mybir.ActivationFunctionType.Sign

P = 128
T, K, N = 8192, 1024, 256
FLOPS = 2 * T * K * N
TILES = T // P
CH = 4
CHUNKS = TILES // CH
WORDS = K // 2
LOADS = (4, 4, 5, 7, 8, 10, 11, 15)
STORES = (24, 24, 8, 4, 4)
assert sum(LOADS) == TILES and sum(STORES) == TILES


def tile_binarylinear_t_kernel(tc, x, weight, out):
    nc = tc.nc
    xv = x.rearrange("(p t) k -> p (t k)", t=TILES)
    ov = out.rearrange("(p t) n -> p (t n)", t=TILES)
    with tc.tile_pool(name="const", bufs=1) as const, tc.tile_pool(name="grp", bufs=2) as grp, tc.tile_pool(
        name="mx", bufs=2
    ) as mx, tc.psum_pool(name="psum", bufs=4) as psum, tc.manual_schedule():
        w_sb = const.tile([P, 2 * K], BF16, name="w_sb")

        def load_w():
            nc.sync.dma_start(
                out=w_sb[:].rearrange("p (j k) -> p j k", j=2),
                in_=weight.rearrange("(j p) k -> p j k", p=P),
            )

        x_words = {}
        first = 0
        for i, n in enumerate(LOADS):
            if i == 0:
                load_w()
            x_sb = const.tile([P, n * K], BF16, name="x_sb%d" % i)
            nc.sync.dma_start(out=x_sb[:], in_=xv[:, first * K : (first + n) * K])
            for t in range(n):
                x_words[first + t] = x_sb[:].bitcast(F32)[:, t * WORDS : (t + 1) * WORDS]
            first += n

        o_slot = {}
        first = 0
        for i, n in enumerate(STORES):
            o_sb = const.tile([P, n * N], F32, name="o_sb%d" % i)
            for t in range(n):
                o_slot[first + t] = (o_sb, t, (first, n) if t == n - 1 else None)
            first += n

        ident = const.tile([P, P], F32, name="ident")
        make_identity(nc, ident[:])

        w_words = w_sb[:].bitcast(F32)
        w_grp = const.tile([P, 4 * 2 * N], BF16, name="w_grp", align_bytes=64)
        w_codes = const.tile([P, 2 * N], U32, name="w_codes", align_bytes=64)
        w_scales = const.tile([P, 2 * N], U8, name="w_scales", align_bytes=64)
        w_grp_v = w_grp[:].rearrange("p (g n u e) -> p g n u e", g=2, n=N, u=2, e=2)

        def weights():
            for jo in range(2):
                wt = psum.tile([P, 512], F32, name="wt", tag="xt")
                for j in range(4):
                    nc.tensor.transpose(
                        wt[:, j * P : (j + 1) * P],
                        w_words[:, jo * WORDS + j * P : jo * WORDS + (j + 1) * P],
                        ident[:],
                    )
                wt_v = wt[:].bitcast(BF16).rearrange("p (g u o e) -> p g o u e", g=2, u=2, o=P, e=2)
                for g in range(2):
                    nc.scalar.activation(out=w_grp_v[:, g, jo * P : (jo + 1) * P, :, :], in_=wt_v[:, g], func=SIGN)
            nc.vector.quantize_mx(out=w_codes[:].bitcast(FP8X4), scales=w_scales[:], in_=w_grp[:])

        grouped = {}
        codes = {}
        scales = {}

        def transposes(c):
            g_sb = grp.tile([P, CH * K], BF16, name="g_sb", tag="g_sb", align_bytes=64)
            grouped[c] = g_sb
            g_words = g_sb[:].bitcast(F32).rearrange("p (r g t u) -> p r g t u", r=CH, g=2, t=P, u=2)
            banks = []
            for r in range(CH):
                xt = psum.tile([P, 512], F32, name="xt", tag="xt")
                for j in range(4):
                    nc.tensor.transpose(xt[:, j * P : (j + 1) * P], x_words[c * CH + r][:, j * P : (j + 1) * P], ident[:])
                banks.append(xt)
            for r in range(CH):
                nc.scalar.copy(
                    out=g_words[:, r],
                    in_=banks[r][:].rearrange("p (g u t) -> p g t u", g=2, u=2, t=P),
                )

        def quantise(c, h):
            if h == 0:
                codes[c] = mx.tile([P, CH * K // 4], U32, name="codes", tag="codes", align_bytes=64)
                scales[c] = mx.tile([P, CH * K // 4], U8, name="scales", tag="scales", align_bytes=64)
            w = CH * K // 8
            nc.vector.quantize_mx(
                out=codes[c][:, h * w : (h + 1) * w].bitcast(FP8X4),
                scales=scales[c][:, h * w : (h + 1) * w],
                in_=grouped[c][:, h * 4 * w : (h + 1) * 4 * w],
            )

        def multiply(c):
            accs = []
            for b in range(CH // 2):
                acc = psum.tile([P, 512], F32, name="acc", tag="acc")
                for half in range(2):
                    r = 2 * b + half
                    for g in range(2):
                        s = (r * 2 + g) * P
                        nc.tensor.matmul_mx(
                            out=acc[:, half * N : (half + 1) * N],
                            lhsT=codes[c][:, s : s + P].bitcast(FP8X4),
                            lhsT_scale=scales[c][:, s : s + P],
                            rhs=w_codes[:, g * N : (g + 1) * N].bitcast(FP8X4),
                            rhs_scale=w_scales[:, g * N : (g + 1) * N],
                            start=(g == 0),
                            stop=(g == 1),
                        )
                accs.append(acc)
            return accs

        def copy_out(c, b, acc):
            t = c * CH + 2 * b
            o_sb, col, unused = o_slot[t]
            nc.vector.tensor_copy(out=o_sb[:, col * N : (col + 2) * N], in_=acc[:])
            store = o_slot[t + 1][2]
            if store is not None:
                nc.sync.dma_start(out=ov[:, store[0] * N : (store[0] + store[1]) * N], in_=o_sb[:])

        weights()
        for c in range(CHUNKS + 1):
            if c < CHUNKS:
                transposes(c)

            accs = multiply(c - 1) if c >= 1 else None
            for h in range(2):
                if c < CHUNKS:
                    quantise(c, h)
                if accs is not None:
                    copy_out(c - 1, h, accs[h])
